import numpy as np
import ml_dtypes


def mxq(x, axis, fmt="e4m3"):
    dtype, down = {"e4m3": (ml_dtypes.float8_e4m3fn, 7), "e5m2": (ml_dtypes.float8_e5m2, 14)}[fmt]
    v = np.moveaxis(np.asarray(x, np.float32).astype(ml_dtypes.bfloat16).astype(np.float64), axis, -1)
    blocks = v.reshape(v.shape[:-1] + (-1, 32))
    amax = np.abs(blocks).max(-1, keepdims=True)
    byte = np.maximum(np.where(amax > 0, np.frexp(amax)[1] - 1 + 127, 0) - down, 1)
    scale = np.exp2(byte - 127.0)
    codes = (blocks / scale).astype(np.float32).astype(dtype).astype(np.float64)
    return np.moveaxis((codes * scale).reshape(v.shape), -1, axis)


WIDE = False


def mx_kscale(k):
    if not WIDE:
        return np.ones(k)
    levels = np.array([20, -20, 10, -10, 0])
    a = np.random.permutation(np.resize(levels, k // 512 * 4)).reshape(k // 512, 4)
    idx = np.arange(k)
    return np.exp2(a[idx // 512, idx % 128 // 32])


BF16 = ml_dtypes.bfloat16


def bf(x):
    return np.asarray(x, np.float32).astype(BF16)


def f64(x):
    return np.asarray(x).astype(np.float64)


S, N, C, O = 9, 2048, 512, 512
K = S * C


def setup_inputs():
    s = mx_kscale(N)[:, None]
    inp = {f"x{i}": bf(np.random.standard_normal((N, C)) * s) for i in range(S)}
    inp["weights"] = bf(np.random.standard_normal((S, O, C)) / np.sqrt(K))
    inp["bias"] = bf(np.random.standard_normal((S, O)) * 0.3)
    g = np.random.standard_normal((N, O)) * np.exp2(np.random.randint(-12, 1, (N, 1))) / s
    inp["grad_out"] = bf(g)
    return inp


def reference(x0, x1, x2, x3, x4, x5, x6, x7, x8, weights, bias, grad_out):
    xs = np.stack([f64(x0), f64(x1), f64(x2), f64(x3), f64(x4), f64(x5), f64(x6), f64(x7), f64(x8)], axis=0)
    gq = mxq(f64(grad_out), 0, "e5m2")
    xq = mxq(xs, 1, "e4m3")
    return np.matmul(gq.T, xq)

@@ -1,0 +1,173 @@
+from contextlib import ExitStack
+
+import concourse.mybir as mybir
+
+BF16 = mybir.dt.bfloat16
+F32 = mybir.dt.float32
+U32 = mybir.dt.uint32
+U8 = mybir.dt.uint8
+E4M3X4 = mybir.dt.float8_e4m3fn_x4
+E5M2X4 = mybir.dt.float8_e5m2_x4
+
+P = 128
+PACK = 4
+SLOTS, TOKENS, C_IN, C_OUT = 9, 2048, 512, 512
+PASSES = TOKENS // (P * PACK)
+O_TILES = C_OUT // P
+UNITS = SLOTS + 1
+
+FLOPS = 2 * SLOTS * TOKENS * C_IN * C_OUT
+BYTES = 2 * UNITS * TOKENS * C_IN + 4 * SLOTS * C_OUT * C_IN
+
+RAW_BUFS = 6
+V_COLS = 320
+V_Q = V_COLS // PACK
+
+
+def tile_scattervertical_kernel(
+    tc, x0, x1, x2, x3, x4, x5, x6, x7, x8, weights, bias, grad_out, out
+):
+    nc = tc.nc
+    sources = [grad_out, x0, x1, x2, x3, x4, x5, x6, x7, x8]
+
+    with ExitStack() as ctx:
+        raw_pool = ctx.enter_context(tc.tile_pool(name="raw", bufs=RAW_BUFS))
+        grp_pool = ctx.enter_context(tc.tile_pool(name="grp", bufs=4))
+        g_pool = ctx.enter_context(tc.tile_pool(name="gq", bufs=1))
+        xq_pool = ctx.enter_context(tc.tile_pool(name="xq", bufs=3))
+        res_pool = ctx.enter_context(tc.tile_pool(name="res", bufs=SLOTS))
+        psum = ctx.enter_context(tc.psum_pool(name="acc", bufs=2))
+        ctx.enter_context(tc.manual_schedule())
+
+        seq = []
+        for c in range(PASSES):
+            seq.append((0, c))
+            seq.append((1, c))
+        for u in range(2, UNITS):
+            for c in range(PASSES):
+                seq.append((u, c))
+        steps = len(seq)
+
+        raw = {}
+        codes = {}
+        planes = {}
+        grouped = {}
+        acc = {}
+        res = {}
+
+        def new_raw(u):
+            raw_t = raw_pool.tile([P, PASSES, PACK, C_IN], BF16, name="raw_t", tag="raw")
+            raw[u] = raw_t
+
+        def load(u, c0, c1):
+            view = sources[u].rearrange("(c p t) w -> p c t w", c=PASSES, p=P, t=PACK)
+            nc.sync.dma_start(out=raw[u][:, c0:c1], in_=view[:, c0:c1])
+
+        def load_unit(u):
+            new_raw(u)
+            load(u, 0, 2)
+            load(u, 2, 4)
+
+        def regroup(i):
+            u, c = seq[i]
+            grp_t = grp_pool.tile([P, C_IN, PACK], BF16, name="grp_t", tag="grp", align_bytes=64)
+            grouped[i] = grp_t
+            if u == 0:
+                dst = grp_t.rearrange("p (m q) t -> p q t m", m=O_TILES)
+                src = raw[u][:, c].rearrange("p t (q m) -> p q t m", m=O_TILES)
+                nc.vector.tensor_copy(out=dst[:, 0:V_Q], in_=src[:, 0:V_Q])
+                nc.scalar.copy(out=dst[:, V_Q:P], in_=src[:, V_Q:P])
+            else:
+                nc.vector.tensor_copy(
+                    out=grp_t[:, 0:V_COLS, :].rearrange("p (b i) t -> p b t i", i=4),
+                    in_=raw[u][:, c, :, 0:V_COLS].rearrange("p t (b i) -> p b t i", i=4),
+                )
+                nc.scalar.copy(
+                    out=grp_t[:, V_COLS:C_IN, :].rearrange("p (b i) t -> p b t i", i=4),
+                    in_=raw[u][:, c, :, V_COLS:C_IN].rearrange("p t (b i) -> p b t i", i=4),
+                )
+
+        def quantise(i):
+            u, c = seq[i]
+            if c == 0:
+                pool = g_pool if u == 0 else xq_pool
+                tag = "g" if u == 0 else "x"
+                codes_t = pool.tile([P, PASSES, C_IN], U32, name="codes_t", tag=tag + "codes", align_bytes=64)
+                planes_t = pool.tile([P, PASSES, C_IN], U8, name="planes_t", tag=tag + "planes", align_bytes=64)
+                codes[u] = codes_t
+                planes[u] = planes_t
+            nc.vector.quantize_mx(
+                out=codes[u][:, c, :].bitcast(E5M2X4 if u == 0 else E4M3X4),
+                scales=planes[u][:, c, :],
+                in_=grouped[i].rearrange("p w t -> p (w t)"),
+            )
+
+        def multiply(i):
+            u, c = seq[i]
+            k = u - 1
+            for m in range(O_TILES):
+                if c == 0:
+                    acc_t = psum.tile([P, C_IN], F32, name="acc_t", tag="acc%d" % m)
+                    acc[(k, m)] = acc_t
+                cols = slice(m * P, (m + 1) * P)
+                nc.tensor.matmul_mx(
+                    out=acc[(k, m)][:],
+                    lhsT=codes[0][:, c, cols].bitcast(E5M2X4),
+                    lhsT_scale=planes[0][:, c, cols],
+                    rhs=codes[u][:, c, :].bitcast(E4M3X4),
+                    rhs_scale=planes[u][:, c, :],
+                    start=(c == 0),
+                    stop=(c == PASSES - 1),
+                )
+
+        def evacuate(k, m, engine):
+            if m == 0:
+                res_t = res_pool.tile([P, O_TILES, C_IN], F32, name="res_t", tag="res")
+                res[k] = res_t
+            if engine == "v":
+                nc.vector.tensor_copy(out=res[k][:, m, :], in_=acc[(k, m)][:])
+            else:
+                nc.scalar.copy(out=res[k][:, m, :], in_=acc[(k, m)][:])
+
+        def store(k):
+            nc.sync.dma_start(
+                out=out[k].rearrange("(q m) c -> q m c", m=O_TILES), in_=res[k][:]
+            )
+
+        new_raw(0)
+        new_raw(1)
+        for c in range(PASSES):
+            load(0, c, c + 1)
+            load(1, c, c + 1)
+        for u in range(2, RAW_BUFS):
+            load_unit(u)
+        next_load = RAW_BUFS
+
+        evac_at = {}
+        ready_stores = []
+        for i in range(steps + 1 + O_TILES + 1):
+            if i < steps:
+                regroup(i)
+            for k, m in evac_at.get(i, []):
+                last = k == SLOTS - 1
+                evacuate(k, m, "v" if (last and m % 2 == 1) else "s")
+                if m == O_TILES - 1:
+                    ready_stores.append(k)
+            if 1 <= i <= steps:
+                quantise(i - 1)
+                u, c = seq[i - 1]
+                if u > 0:
+                    multiply(i - 1)
+                    if c == PASSES - 1:
+                        for m in range(O_TILES):
+                            at = i + 1 + (m if u < UNITS - 1 else 0)
+                            evac_at[at] = evac_at.get(at, []) + [(u - 1, m)]
+            if i < steps:
+                u, c = seq[i]
+                if c == PASSES - 1 and next_load < UNITS:
+                    load_unit(next_load)
+                    next_load += 1
+            if next_load == UNITS:
+                for k in ready_stores:
+                    store(k)
+                ready_stores = []

@@ -65,8 +65,7 @@ def tile_scattervertical_kernel(
 
         def load_unit(u):
             new_raw(u)
-            load(u, 0, 2)
-            load(u, 2, 4)
+            load(u, 0, PASSES)
 
         def regroup(i):
             u, c = seq[i]

@@ -56,7 +56,7 @@ def tile_scattervertical_kernel(
         res = {}
 
         def new_raw(u):
-            raw_t = raw_pool.tile([P, PASSES, PACK, C_IN], BF16, name="raw_t", tag="raw")
+            raw_t = raw_pool.tile([P, PASSES, PACK, C_IN], BF16, name="raw_t", tag="raw", align_bytes=256)
             raw[u] = raw_t
 
         def load(u, c0, c1):
@@ -121,7 +121,7 @@ def tile_scattervertical_kernel(
 
         def evacuate(k, m, engine):
             if m == 0:
-                res_t = res_pool.tile([P, O_TILES, C_IN], F32, name="res_t", tag="res")
+                res_t = res_pool.tile([P, O_TILES, C_IN], F32, name="res_t", tag="res", align_bytes=256)
                 res[k] = res_t
             if engine == "v":
                 nc.vector.tensor_copy(out=res[k][:, m, :], in_=acc[(k, m)][:])

@@ -56,7 +56,7 @@ def tile_scattervertical_kernel(
         res = {}
 
         def new_raw(u):
-            raw_t = raw_pool.tile([P, PASSES, PACK, C_IN], BF16, name="raw_t", tag="raw", align_bytes=256)
+            raw_t = raw_pool.tile([P, PASSES, PACK, C_IN], BF16, name="raw_t", tag="raw", align_bytes=4096)
             raw[u] = raw_t
 
         def load(u, c0, c1):
@@ -121,7 +121,7 @@ def tile_scattervertical_kernel(
 
         def evacuate(k, m, engine):
             if m == 0:
-                res_t = res_pool.tile([P, O_TILES, C_IN], F32, name="res_t", tag="res", align_bytes=256)
+                res_t = res_pool.tile([P, O_TILES, C_IN], F32, name="res_t", tag="res", align_bytes=4096)
                 res[k] = res_t
             if engine == "v":
                 nc.vector.tensor_copy(out=res[k][:, m, :], in_=acc[(k, m)][:])

@@ -22,6 +22,7 @@ BYTES = 2 * UNITS * TOKENS * C_IN + 4 * SLOTS * C_OUT * C_IN
 RAW_BUFS = 6
 V_COLS = 320
 V_Q = V_COLS // PACK
+PAIRED = 6
 
 
 def tile_scattervertical_kernel(
@@ -35,7 +36,7 @@ def tile_scattervertical_kernel(
         grp_pool = ctx.enter_context(tc.tile_pool(name="grp", bufs=4))
         g_pool = ctx.enter_context(tc.tile_pool(name="gq", bufs=1))
         xq_pool = ctx.enter_context(tc.tile_pool(name="xq", bufs=3))
-        res_pool = ctx.enter_context(tc.tile_pool(name="res", bufs=SLOTS))
+        res_pool = ctx.enter_context(tc.tile_pool(name="res", bufs=3))
         psum = ctx.enter_context(tc.psum_pool(name="acc", bufs=2))
         ctx.enter_context(tc.manual_schedule())
 
@@ -54,6 +55,7 @@ def tile_scattervertical_kernel(
         grouped = {}
         acc = {}
         res = {}
+        pairs = {}
 
         def new_raw(u):
             raw_t = raw_pool.tile([P, PASSES, PACK, C_IN], BF16, name="raw_t", tag="raw", align_bytes=4096)
@@ -120,7 +122,12 @@ def tile_scattervertical_kernel(
                 )
 
         def evacuate(k, m, engine):
-            if m == 0:
+            if m == 0 and k < PAIRED and k % 2 == 0:
+                pair_t = res_pool.tile([P, 2, O_TILES, C_IN], F32, name="pair_t", tag="pair", align_bytes=4096)
+                pairs[k] = pair_t
+                res[k] = pair_t[:, 0]
+                res[k + 1] = pair_t[:, 1]
+            if m == 0 and k >= PAIRED:
                 res_t = res_pool.tile([P, O_TILES, C_IN], F32, name="res_t", tag="res", align_bytes=4096)
                 res[k] = res_t
             if engine == "v":
@@ -129,9 +136,14 @@ def tile_scattervertical_kernel(
                 nc.scalar.copy(out=res[k][:, m, :], in_=acc[(k, m)][:])
 
         def store(k):
-            nc.sync.dma_start(
-                out=out[k].rearrange("(q m) c -> q m c", m=O_TILES), in_=res[k][:]
-            )
+            if k >= PAIRED:
+                nc.sync.dma_start(
+                    out=out[k].rearrange("(q m) c -> q m c", m=O_TILES), in_=res[k][:]
+                )
+            elif k % 2 == 1:
+                nc.sync.dma_start(
+                    out=out[k - 1 : k + 1].rearrange("s (q m) c -> q s m c", m=O_TILES), in_=pairs[k - 1][:]
+                )
 
         new_raw(0)
         new_raw(1)

@@ -23,6 +23,8 @@ RAW_BUFS = 6
 V_COLS = 320
 V_Q = V_COLS // PACK
 PAIRED = 6
+SPLIT = O_TILES * C_IN - 384
+SMALL_AFTER = {1: range(0, 5), 3: range(5, 10), 5: range(10, 16)}
 
 
 def tile_scattervertical_kernel(
@@ -140,10 +142,24 @@ def tile_scattervertical_kernel(
                 nc.sync.dma_start(
                     out=out[k].rearrange("(q m) c -> q m c", m=O_TILES), in_=res[k][:]
                 )
+            elif k == 1:
+                nc.sync.dma_start(
+                    out=out[0].rearrange("(q m) c -> q (m c)", m=O_TILES)[:, 0:SPLIT],
+                    in_=res[0].rearrange("q m c -> q (m c)")[:, 0:SPLIT],
+                )
+                nc.sync.dma_start(out=out[1].rearrange("(q m) c -> q m c", m=O_TILES), in_=res[1])
             elif k % 2 == 1:
                 nc.sync.dma_start(
                     out=out[k - 1 : k + 1].rearrange("s (q m) c -> q s m c", m=O_TILES), in_=pairs[k - 1][:]
                 )
+
+        def store_small(j):
+            first = 32 * (j % 4) + j // 4
+            rows = slice(first, 32 * (j % 4) + 32, 4)
+            nc.sync.dma_start(
+                out=out[0].rearrange("(q m) c -> q (m c)", m=O_TILES)[rows, SPLIT:],
+                in_=res[0].rearrange("q m c -> q (m c)")[rows, SPLIT:],
+            )
 
         new_raw(0)
         new_raw(1)
@@ -181,4 +197,6 @@ def tile_scattervertical_kernel(
             if next_load == UNITS:
                 for k in ready_stores:
                     store(k)
+                    for j in SMALL_AFTER.get(k, []):
+                        store_small(j)
                 ready_stores = []

from contextlib import ExitStack

import concourse.mybir as mybir

BF16 = mybir.dt.bfloat16
F32 = mybir.dt.float32
U32 = mybir.dt.uint32
U8 = mybir.dt.uint8
E4M3X4 = mybir.dt.float8_e4m3fn_x4
E5M2X4 = mybir.dt.float8_e5m2_x4

P = 128
PACK = 4
SLOTS, TOKENS, C_IN, C_OUT = 9, 2048, 512, 512
PASSES = TOKENS // (P * PACK)
O_TILES = C_OUT // P
UNITS = SLOTS + 1

FLOPS = 2 * SLOTS * TOKENS * C_IN * C_OUT
BYTES = 2 * UNITS * TOKENS * C_IN + 4 * SLOTS * C_OUT * C_IN

RAW_BUFS = 6
V_COLS = 320
V_Q = V_COLS // PACK
PAIRED = 6
SPLIT = O_TILES * C_IN - 384
SMALL_AFTER = {1: range(0, 5), 3: range(5, 10), 5: range(10, 16)}


def tile_scattervertical_kernel(
    tc, x0, x1, x2, x3, x4, x5, x6, x7, x8, weights, bias, grad_out, out
):
    nc = tc.nc
    sources = [grad_out, x0, x1, x2, x3, x4, x5, x6, x7, x8]

    with ExitStack() as ctx:
        raw_pool = ctx.enter_context(tc.tile_pool(name="raw", bufs=RAW_BUFS))
        grp_pool = ctx.enter_context(tc.tile_pool(name="grp", bufs=4))
        g_pool = ctx.enter_context(tc.tile_pool(name="gq", bufs=1))
        xq_pool = ctx.enter_context(tc.tile_pool(name="xq", bufs=3))
        res_pool = ctx.enter_context(tc.tile_pool(name="res", bufs=3))
        psum = ctx.enter_context(tc.psum_pool(name="acc", bufs=2))
        ctx.enter_context(tc.manual_schedule())

        seq = []
        for c in range(PASSES):
            seq.append((0, c))
            seq.append((1, c))
        for u in range(2, UNITS):
            for c in range(PASSES):
                seq.append((u, c))
        steps = len(seq)

        raw = {}
        codes = {}
        planes = {}
        grouped = {}
        acc = {}
        res = {}
        pairs = {}

        def new_raw(u):
            raw_t = raw_pool.tile([P, PASSES, PACK, C_IN], BF16, name="raw_t", tag="raw", align_bytes=4096)
            raw[u] = raw_t

        def load(u, c0, c1):
            view = sources[u].rearrange("(c p t) w -> p c t w", c=PASSES, p=P, t=PACK)
            nc.sync.dma_start(out=raw[u][:, c0:c1], in_=view[:, c0:c1])

        def load_unit(u):
            new_raw(u)
            load(u, 0, PASSES)

        def regroup(i):
            u, c = seq[i]
            grp_t = grp_pool.tile([P, C_IN, PACK], BF16, name="grp_t", tag="grp", align_bytes=64)
            grouped[i] = grp_t
            if u == 0:
                dst = grp_t.rearrange("p (m q) t -> p q t m", m=O_TILES)
                src = raw[u][:, c].rearrange("p t (q m) -> p q t m", m=O_TILES)
                nc.vector.tensor_copy(out=dst[:, 0:V_Q], in_=src[:, 0:V_Q])
                nc.scalar.copy(out=dst[:, V_Q:P], in_=src[:, V_Q:P])
            else:
                nc.vector.tensor_copy(
                    out=grp_t[:, 0:V_COLS, :].rearrange("p (b i) t -> p b t i", i=4),
                    in_=raw[u][:, c, :, 0:V_COLS].rearrange("p t (b i) -> p b t i", i=4),
                )
                nc.scalar.copy(
                    out=grp_t[:, V_COLS:C_IN, :].rearrange("p (b i) t -> p b t i", i=4),
                    in_=raw[u][:, c, :, V_COLS:C_IN].rearrange("p t (b i) -> p b t i", i=4),
                )

        def quantise(i):
            u, c = seq[i]
            if c == 0:
                pool = g_pool if u == 0 else xq_pool
                tag = "g" if u == 0 else "x"
                codes_t = pool.tile([P, PASSES, C_IN], U32, name="codes_t", tag=tag + "codes", align_bytes=64)
                planes_t = pool.tile([P, PASSES, C_IN], U8, name="planes_t", tag=tag + "planes", align_bytes=64)
                codes[u] = codes_t
                planes[u] = planes_t
            nc.vector.quantize_mx(
                out=codes[u][:, c, :].bitcast(E5M2X4 if u == 0 else E4M3X4),
                scales=planes[u][:, c, :],
                in_=grouped[i].rearrange("p w t -> p (w t)"),
            )

        def multiply(i):
            u, c = seq[i]
            k = u - 1
            for m in range(O_TILES):
                if c == 0:
                    acc_t = psum.tile([P, C_IN], F32, name="acc_t", tag="acc%d" % m)
                    acc[(k, m)] = acc_t
                cols = slice(m * P, (m + 1) * P)
                nc.tensor.matmul_mx(
                    out=acc[(k, m)][:],
                    lhsT=codes[0][:, c, cols].bitcast(E5M2X4),
                    lhsT_scale=planes[0][:, c, cols],
                    rhs=codes[u][:, c, :].bitcast(E4M3X4),
                    rhs_scale=planes[u][:, c, :],
                    start=(c == 0),
                    stop=(c == PASSES - 1),
                )

        def evacuate(k, m, engine):
            if m == 0 and k < PAIRED and k % 2 == 0:
                pair_t = res_pool.tile([P, 2, O_TILES, C_IN], F32, name="pair_t", tag="pair", align_bytes=4096)
                pairs[k] = pair_t
                res[k] = pair_t[:, 0]
                res[k + 1] = pair_t[:, 1]
            if m == 0 and k >= PAIRED:
                res_t = res_pool.tile([P, O_TILES, C_IN], F32, name="res_t", tag="res", align_bytes=4096)
                res[k] = res_t
            if engine == "v":
                nc.vector.tensor_copy(out=res[k][:, m, :], in_=acc[(k, m)][:])
            else:
                nc.scalar.copy(out=res[k][:, m, :], in_=acc[(k, m)][:])

        def store(k):
            if k >= PAIRED:
                nc.sync.dma_start(
                    out=out[k].rearrange("(q m) c -> q m c", m=O_TILES), in_=res[k][:]
                )
            elif k == 1:
                nc.sync.dma_start(
                    out=out[0].rearrange("(q m) c -> q (m c)", m=O_TILES)[:, 0:SPLIT],
                    in_=res[0].rearrange("q m c -> q (m c)")[:, 0:SPLIT],
                )
                nc.sync.dma_start(out=out[1].rearrange("(q m) c -> q m c", m=O_TILES), in_=res[1])
            elif k % 2 == 1:
                nc.sync.dma_start(
                    out=out[k - 1 : k + 1].rearrange("s (q m) c -> q s m c", m=O_TILES), in_=pairs[k - 1][:]
                )

        def store_small(j):
            first = 32 * (j % 4) + j // 4
            rows = slice(first, 32 * (j % 4) + 32, 4)
            nc.sync.dma_start(
                out=out[0].rearrange("(q m) c -> q (m c)", m=O_TILES)[rows, SPLIT:],
                in_=res[0].rearrange("q m c -> q (m c)")[rows, SPLIT:],
            )

        new_raw(0)
        new_raw(1)
        for c in range(PASSES):
            load(0, c, c + 1)
            load(1, c, c + 1)
        for u in range(2, RAW_BUFS):
            load_unit(u)
        next_load = RAW_BUFS

        evac_at = {}
        ready_stores = []
        for i in range(steps + 1 + O_TILES + 1):
            if i < steps:
                regroup(i)
            for k, m in evac_at.get(i, []):
                last = k == SLOTS - 1
                evacuate(k, m, "v" if (last and m % 2 == 1) else "s")
                if m == O_TILES - 1:
                    ready_stores.append(k)
            if 1 <= i <= steps:
                quantise(i - 1)
                u, c = seq[i - 1]
                if u > 0:
                    multiply(i - 1)
                    if c == PASSES - 1:
                        for m in range(O_TILES):
                            at = i + 1 + (m if u < UNITS - 1 else 0)
                            evac_at[at] = evac_at.get(at, []) + [(u - 1, m)]
            if i < steps:
                u, c = seq[i]
                if c == PASSES - 1 and next_load < UNITS:
                    load_unit(next_load)
                    next_load += 1
            if next_load == UNITS:
                for k in ready_stores:
                    store(k)
                    for j in SMALL_AFTER.get(k, []):
                        store_small(j)
                ready_stores = []
